import numpy as np
import ml_dtypes


def mxq(x, axis, fmt="e4m3"):
    dtype, down = {"e4m3": (ml_dtypes.float8_e4m3fn, 7), "e5m2": (ml_dtypes.float8_e5m2, 14)}[fmt]
    v = np.moveaxis(np.asarray(x, np.float32).astype(ml_dtypes.bfloat16).astype(np.float64), axis, -1)
    blocks = v.reshape(v.shape[:-1] + (-1, 32))
    amax = np.abs(blocks).max(-1, keepdims=True)
    byte = np.maximum(np.where(amax > 0, np.frexp(amax)[1] - 1 + 127, 0) - down, 1)
    scale = np.exp2(byte - 127.0)
    codes = (blocks / scale).astype(np.float32).astype(dtype).astype(np.float64)
    return np.moveaxis((codes * scale).reshape(v.shape), -1, axis)


WIDE = False


def mx_kscale(k):
    if not WIDE:
        return np.ones(k)
    levels = np.array([18, -18])
    if k % 512:
        return np.exp2(np.random.permutation(np.resize(levels, k // 32))).repeat(32)
    a = np.empty((k // 512, 16))
    for p in range(k // 512):
        a[p, :8] = np.random.permutation(np.resize(levels, 8))
        for g in range(8):
            far = levels[np.abs(levels - a[p, g]) >= 10]
            a[p, g + 8] = far[np.random.randint(len(far))]
    return np.exp2(a.ravel()).repeat(32)


BF16 = ml_dtypes.bfloat16


def bf(x):
    return np.asarray(x, np.float32).astype(BF16)


def f64(x):
    return np.asarray(x).astype(np.float64)


N, NK, D_IN, D_H, D_V = 1024, 1024, 512, 512, 512


def softmax_rows(sc):
    e = np.exp(sc - sc.max(-1, keepdims=True))
    return e / e.sum(-1, keepdims=True)


def setup_inputs():
    u = mx_kscale(N)
    v = mx_kscale(D_V)
    s = mx_kscale(NK)
    uu = u / np.min(u)
    ss = s / np.min(s)
    vv = v / np.max(v)
    c = np.min(s)
    q = bf(np.random.standard_normal((N, D_H)) * 1.4)
    k = bf(np.random.standard_normal((N, D_H)) * 1.4)
    h0 = bf(np.random.standard_normal((N, D_H)) * 1.1)
    cooccur0 = bf(np.random.standard_normal((N, N)) * 0.5 / np.sqrt(N))
    wv0 = bf(np.random.standard_normal((D_H, D_H)) * 2.7 / np.sqrt(D_H))
    bv = bf(np.random.standard_normal(D_H) * 0.3)
    p = softmax_rows(f64(q) @ f64(k).T / np.sqrt(D_H))
    y = (p + f64(cooccur0)) @ (f64(h0) @ f64(wv0).T + f64(bv))
    g = bf(np.random.standard_normal((N, D_V)) * np.exp2(np.random.randint(-6, 1, (N, 1))) / uu[:, None] * vv[None, :] * c)
    return {
        "q": q,
        "k": k,
        "h": bf(f64(h0) / ss[:, None]),
        "cooccur": bf(f64(cooccur0) * uu[:, None] * ss[None, :]),
        "wv": bf(f64(wv0) / vv[:, None]),
        "bv": bv,
        "p": np.asarray(p, np.float32),
        "y": np.asarray(y, np.float32),
        "grad_out": g,
    }


def reference(q, k, h, cooccur, wv, bv, p, y, grad_out):
    g = f64(grad_out)
    dz2 = g * (f64(y) > 0.0)
    att = f64(p) + f64(cooccur)
    dz1 = mxq(att, 0, "e4m3").T @ mxq(dz2, 0, "e5m2")
    dh = (mxq(dz1, 1, "e5m2") @ mxq(f64(wv), 0, "e4m3")) + g
    dwv = mxq(dz1, 0, "e5m2").T @ mxq(f64(h), 0, "e4m3")
    return dh, dwv

@@ -1,0 +1,249 @@
+from contextlib import ExitStack
+
+import concourse.mybir as mybir
+from concourse.masks import make_identity
+
+N = 1024
+D = 512
+P = 128
+J = 4
+G = 512
+
+F32 = mybir.dt.float32
+BF16 = mybir.dt.bfloat16
+U32 = mybir.dt.uint32
+U8 = mybir.dt.uint8
+E4M3 = mybir.dt.float8_e4m3fn_x4
+E5M2 = mybir.dt.float8_e5m2_x4
+ALU = mybir.AluOpType
+
+FLOPS = 2 * N * N * D + 2 * 2 * N * D * D
+BYTES = N * D * 2 * 2 + N * N * 2 + D * D * 2 + N * N * 4 + N * D * 4 + N * D * 4 + D * D * 4
+
+
+def tile_semanticgraph_pb_v_kernel(tc, q, k, h, cooccur, wv, bv, p, y, grad_out, out_0, out_1):
+    nc = tc.nc
+    with ExitStack() as ctx:
+        keep = ctx.enter_context(tc.tile_pool(name="keep", bufs=1))
+        psum = ctx.enter_context(tc.psum_pool(name="psum", bufs=1))
+
+        def sb(shape, dtype, name):
+            return keep.tile(shape, dtype, name=name, align_bytes=64)
+
+        def bank(shape, name):
+            return psum.tile(shape, F32, name=name)
+
+        ctx.enter_context(tc.manual_schedule())
+
+        def load(ap, shape, dtype, name):
+            t = sb(shape, dtype, name)
+            nc.sync.dma_start(out=t[:], in_=ap)
+            return t
+
+        def rows(ap, i, c0, c1):
+            return ap[G * i : G * (i + 1), c0:c1].rearrange("(p j) w -> p j w", j=J)
+
+        def load_p(i, hf):
+            return load(rows(p, i, G * hf, G * (hf + 1)), [P, J, G], F32, f"p_{i}{hf}")
+
+        def load_c(i, hf):
+            return load(rows(cooccur, i, G * hf, G * (hf + 1)), [P, J, G], BF16, f"c_{i}{hf}")
+
+        g_raw, y_raw, p_raw, c_raw = {}, {}, {}, {}
+        y_raw[0, 0] = load(rows(y, 0, 0, 256), [P, J, 256], F32, "y_00")
+        g_raw[0] = load(rows(grad_out, 0, 0, D), [P, J, D], BF16, "g_0")
+        y_raw[0, 1] = load(rows(y, 0, 256, 512), [P, J, 256], F32, "y_01")
+        c_raw[0, 0] = load_c(0, 0)
+        p_raw[0, 0] = load_p(0, 0)
+        g_raw[1] = load(rows(grad_out, 1, 0, D), [P, J, D], BF16, "g_1")
+        y_raw[1] = load(rows(y, 1, 0, D), [P, J, D], F32, "y_1")
+        c_raw[1, 0] = load_c(1, 0)
+        p_raw[1, 0] = load_p(1, 0)
+        wv_raw = load(rows(wv, 0, 0, D), [P, J, D], BF16, "wv_raw")
+        c_raw[0, 1] = load_c(0, 1)
+        p_raw[0, 1] = load_p(0, 1)
+        c_raw[1, 1] = load_c(1, 1)
+        p_raw[1, 1] = load_p(1, 1)
+        h_raw = [load(rows(h, i, 0, D), [P, J, D], BF16, f"h_raw{i}") for i in range(2)]
+
+        ident = sb([P, P], F32, "ident")
+        make_identity(nc, ident[:])
+
+        def operand(width, name):
+            return (sb([P, width], U32, name + "_codes"), sb([P, width], U8, name + "_scales"))
+
+        def quantize(op, fmt, grouped, c0, c1):
+            codes, scales = op
+            nc.vector.quantize_mx(
+                out=codes[:, c0:c1].bitcast(fmt), scales=scales[:, c0:c1], in_=grouped[:, J * c0 : J * c1]
+            )
+
+        dz2 = [sb([P, J, D], BF16, f"dz2_{i}") for i in range(2)]
+        dz2_g = [sb([P, D * J], BF16, f"dz2_g{i}") for i in range(2)]
+        dz2_q = [operand(D, f"dz2_q{i}") for i in range(2)]
+        att_g = {(i, hf): sb([P, G * J], BF16, f"att_g{i}{hf}") for i in range(2) for hf in range(2)}
+        att_q = {(i, hf): operand(G, f"att_q{i}{hf}") for i in range(2) for hf in range(2)}
+        wv_g = sb([P, D * J], BF16, "wv_g")
+        wv_q = operand(D, "wv_q")
+        h_g = [sb([P, D * J], BF16, f"h_g{i}") for i in range(2)]
+        h_q = [operand(D, f"h_q{i}") for i in range(2)]
+        dz1 = [sb([P, J, D], BF16, f"dz1_{hf}") for hf in range(2)]
+        dk_g = [sb([P, G * J], BF16, f"dk_g{hf}") for hf in range(2)]
+        dk_q = [operand(G, f"dk_q{hf}") for hf in range(2)]
+        dv_g = [sb([P, D * J], BF16, f"dv_g{hf}") for hf in range(2)]
+        dv_q = [operand(D, f"dv_q{hf}") for hf in range(2)]
+        o0 = [sb([P, J, D], F32, f"o0_{hf}") for hf in range(2)]
+        o1 = sb([P, J, D], F32, "o1")
+
+        def relu_grad(i, yt, c0, c1):
+            nc.vector.scalar_tensor_tensor(
+                out=dz2[i][:, :, c0:c1],
+                in0=yt,
+                scalar=0.0,
+                in1=g_raw[i][:, :, c0:c1],
+                op0=ALU.is_gt,
+                op1=ALU.mult,
+            )
+            interleave(scopy, dz2_g[i], dz2[i], c0, c1)
+
+        def add_att(i, hf, m0, m1):
+            nc.vector.tensor_tensor(
+                out=att_g[i, hf][:].rearrange("p (t m j) -> p m j t", t=4, j=J)[:, m0:m1],
+                in0=p_raw[i, hf][:].rearrange("p j (m t) -> p m j t", t=4)[:, m0:m1],
+                in1=c_raw[i, hf][:].rearrange("p j (m t) -> p m j t", t=4)[:, m0:m1],
+                op=ALU.add,
+            )
+
+        def interleave(engine_copy, dst, src, c0, c1):
+            engine_copy(
+                out=dst[:, J * c0 : J * c1].rearrange("p (c i j) -> p c j i", i=4, j=J),
+                in_=src[:, :, c0:c1].rearrange("p j (c i) -> p c j i", i=4),
+            )
+
+        def mm(out, a, a_fmt, a0, b, b_fmt, start, stop):
+            nc.tensor.matmul_mx(
+                out=out,
+                lhsT=a[0][:, a0 : a0 + P].bitcast(a_fmt),
+                lhsT_scale=a[1][:, a0 : a0 + P],
+                rhs=b[0][:].bitcast(b_fmt),
+                rhs_scale=b[1][:],
+                start=start,
+                stop=stop,
+            )
+
+        acc = {}
+
+        def stage1(hf, i, ts):
+            for t in ts:
+                if i == 0:
+                    acc[hf, t] = bank([P, D], f"acc{t}")
+                mm(acc[hf, t][:], att_q[i, hf], E4M3, P * t, dz2_q[i], E5M2, i == 0, i == 1)
+
+        def evac1(copy, hf, t):
+            copy(out=dz1[hf][:, t, :], in_=acc[hf, t][:])
+
+        tb = {}
+
+        def turn(hf, b):
+            tb[hf, b] = bank([P, 2, 2, P], f"turn{b}")
+            for a in range(2):
+                words = dz1[hf][:, 2 * b + a, :].bitcast(F32)
+                for u in range(2):
+                    nc.tensor.transpose(tb[hf, b][:, a, u, :], words[:, u::2], ident[:])
+
+        def turn_out(hf, b):
+            nc.scalar.copy(
+                out=dk_g[hf][:, 2 * P * J * b : 2 * P * J * (b + 1)].bitcast(F32).rearrange("p (a r u) -> p a r u", a=2, u=2),
+                in_=tb[hf, b][:].rearrange("p a u r -> p a r u"),
+            )
+
+        ob = {}
+
+        def stage2a(hf, t):
+            ob[hf, t] = bank([P, D], f"ob{t % 2}")
+            mm(ob[hf, t][:], dk_q[hf], E5M2, P * t, wv_q, E4M3, True, True)
+
+        def evac2a(hf, t):
+            nc.vector.tensor_tensor(out=o0[hf][:, t, :], in0=ob[hf, t][:], in1=g_raw[hf][:, t, :], op=ALU.add)
+
+        def store_out0(hf, t0, t1):
+            nc.sync.dma_start(out=rows(out_0, hf, 0, D)[:, t0:t1, :], in_=o0[hf][:, t0:t1, :])
+
+        vcopy, scopy = nc.vector.tensor_copy, nc.scalar.copy
+
+        relu_grad(0, y_raw[0, 0][:], 0, 256)
+        relu_grad(0, y_raw[0, 1][:], 256, 512)
+        quantize(dz2_q[0], E5M2, dz2_g[0], 0, D)
+        add_att(0, 0, 0, P)
+        quantize(att_q[0, 0], E4M3, att_g[0, 0], 0, G)
+        stage1(0, 0, range(4))
+        relu_grad(1, y_raw[1][:], 0, D)
+        quantize(dz2_q[1], E5M2, dz2_g[1], 0, D)
+        add_att(1, 0, 0, P)
+        quantize(att_q[1, 0], E4M3, att_g[1, 0], 0, G)
+        stage1(0, 1, range(4))
+        interleave(scopy, wv_g, wv_raw, 0, D)
+        for t in range(4):
+            evac1(scopy, 0, t)
+        quantize(wv_q, E4M3, wv_g, 0, D)
+        add_att(0, 1, 0, P)
+        turn(0, 0)
+        turn(0, 1)
+        turn_out(0, 0)
+        turn_out(0, 1)
+        interleave(scopy, dv_g[0], dz1[0], 0, D)
+        quantize(dk_q[0], E5M2, dk_g[0], 0, 256)
+        quantize(att_q[0, 1], E4M3, att_g[0, 1], 0, G)
+        stage2a(0, 0)
+        stage2a(0, 1)
+        stage1(1, 0, range(4))
+        quantize(dk_q[0], E5M2, dk_g[0], 256, 512)
+        evac2a(0, 0)
+        evac2a(0, 1)
+        stage2a(0, 2)
+        stage2a(0, 3)
+        add_att(1, 1, 0, 64)
+        quantize(dv_q[0], E5M2, dv_g[0], 0, D)
+        add_att(1, 1, 64, P)
+        evac2a(0, 2)
+        quantize(att_q[1, 1], E4M3, att_g[1, 1], 0, 256)
+        quantize(att_q[1, 1], E4M3, att_g[1, 1], 256, 512)
+        stage1(1, 1, range(4))
+        evac2a(0, 3)
+        store_out0(0, 0, 4)
+        interleave(scopy, h_g[0], h_raw[0], 0, D)
+        evac1(scopy, 1, 0)
+        evac1(vcopy, 1, 1)
+        evac1(scopy, 1, 2)
+        evac1(vcopy, 1, 3)
+        turn(1, 0)
+        turn(1, 1)
+        quantize(h_q[0], E4M3, h_g[0], 0, D)
+        turn_out(1, 0)
+        turn_out(1, 1)
+        interleave(vcopy, dv_g[1], dz1[1], 0, 256)
+        quantize(dk_q[1], E5M2, dk_g[1], 0, 256)
+        stage2a(1, 0)
+        stage2a(1, 1)
+        interleave(scopy, h_g[1], h_raw[1], 0, D)
+        interleave(vcopy, dv_g[1], dz1[1], 256, 512)
+        quantize(dk_q[1], E5M2, dk_g[1], 256, 512)
+        quantize(dv_q[1], E5M2, dv_g[1], 0, D)
+        evac2a(1, 0)
+        evac2a(1, 1)
+        store_out0(1, 0, 2)
+        stage2a(1, 2)
+        stage2a(1, 3)
+        quantize(h_q[1], E4M3, h_g[1], 0, D)
+        evac2a(1, 2)
+        evac2a(1, 3)
+        store_out0(1, 2, 4)
+        for c in range(4):
+            wb = bank([P, D], f"acc{c}")
+            for i in range(2):
+                mm(wb[:], dv_q[i], E5M2, P * c, h_q[i], E4M3, i == 0, i == 1)
+            (scopy if c % 2 == 0 else vcopy)(out=o1[:, c, :], in_=wb[:])
+            if c % 2 == 1:
+                nc.sync.dma_start(
+                    out=out_1[P * (c - 1) : P * (c + 1), :].rearrange("(c p) w -> p c w", p=P), in_=o1[:, c - 1 : c + 1, :]
+                )

@@ -47,24 +47,25 @@ def tile_semanticgraph_pb_v_kernel(tc, q, k, h, cooccur, wv, bv, p, y, grad_out,
             return load(rows(p, i, G * hf, G * (hf + 1)), [P, J, G], F32, f"p_{i}{hf}")
 
         def load_c(i, hf):
-            return load(rows(cooccur, i, G * hf, G * (hf + 1)), [P, J, G], BF16, f"c_{i}{hf}")
+            return load(rows(cooccur, i, G * hf, G * (hf + 1)), [P, J, G], BF16, f"c_{i}{hf}")[:]
 
         g_raw, y_raw, p_raw, c_raw = {}, {}, {}, {}
-        y_raw[0, 0] = load(rows(y, 0, 0, 256), [P, J, 256], F32, "y_00")
+        h_raw = {}
+        y_raw[0] = load(rows(y, 0, 0, D), [P, J, D], F32, "y_0")
         g_raw[0] = load(rows(grad_out, 0, 0, D), [P, J, D], BF16, "g_0")
-        y_raw[0, 1] = load(rows(y, 0, 256, 512), [P, J, 256], F32, "y_01")
         c_raw[0, 0] = load_c(0, 0)
         p_raw[0, 0] = load_p(0, 0)
-        g_raw[1] = load(rows(grad_out, 1, 0, D), [P, J, D], BF16, "g_1")
         y_raw[1] = load(rows(y, 1, 0, D), [P, J, D], F32, "y_1")
+        g_raw[1] = load(rows(grad_out, 1, 0, D), [P, J, D], BF16, "g_1")
         c_raw[1, 0] = load_c(1, 0)
         p_raw[1, 0] = load_p(1, 0)
         wv_raw = load(rows(wv, 0, 0, D), [P, J, D], BF16, "wv_raw")
         c_raw[0, 1] = load_c(0, 1)
         p_raw[0, 1] = load_p(0, 1)
+        h_raw[0] = load(rows(h, 0, 0, D), [P, J, D], BF16, "h_raw0")
         c_raw[1, 1] = load_c(1, 1)
         p_raw[1, 1] = load_p(1, 1)
-        h_raw = [load(rows(h, i, 0, D), [P, J, D], BF16, f"h_raw{i}") for i in range(2)]
+        h_raw[1] = load(rows(h, 1, 0, D), [P, J, D], BF16, "h_raw1")
 
         ident = sb([P, P], F32, "ident")
         make_identity(nc, ident[:])
@@ -104,13 +105,13 @@ def tile_semanticgraph_pb_v_kernel(tc, q, k, h, cooccur, wv, bv, p, y, grad_out,
                 op0=ALU.is_gt,
                 op1=ALU.mult,
             )
-            interleave(scopy, dz2_g[i], dz2[i], c0, c1)
+
 
         def add_att(i, hf, m0, m1):
             nc.vector.tensor_tensor(
                 out=att_g[i, hf][:].rearrange("p (t m j) -> p m j t", t=4, j=J)[:, m0:m1],
                 in0=p_raw[i, hf][:].rearrange("p j (m t) -> p m j t", t=4)[:, m0:m1],
-                in1=c_raw[i, hf][:].rearrange("p j (m t) -> p m j t", t=4)[:, m0:m1],
+                in1=c_raw[i, hf].rearrange("p j (m t) -> p m j t", t=4)[:, m0:m1],
                 op=ALU.add,
             )
 
@@ -160,7 +161,7 @@ def tile_semanticgraph_pb_v_kernel(tc, q, k, h, cooccur, wv, bv, p, y, grad_out,
         ob = {}
 
         def stage2a(hf, t):
-            ob[hf, t] = bank([P, D], f"ob{t % 2}")
+            ob[hf, t] = bank([P, D], f"turn{t - 2}" if (hf, t // 2) == (1, 1) else f"ob{t % 2}")
             mm(ob[hf, t][:], dk_q[hf], E5M2, P * t, wv_q, E4M3, True, True)
 
         def evac2a(hf, t):
@@ -170,80 +171,123 @@ def tile_semanticgraph_pb_v_kernel(tc, q, k, h, cooccur, wv, bv, p, y, grad_out,
             nc.sync.dma_start(out=rows(out_0, hf, 0, D)[:, t0:t1, :], in_=o0[hf][:, t0:t1, :])
 
         vcopy, scopy = nc.vector.tensor_copy, nc.scalar.copy
+        wb = {}
 
-        relu_grad(0, y_raw[0, 0][:], 0, 256)
-        relu_grad(0, y_raw[0, 1][:], 256, 512)
-        quantize(dz2_q[0], E5M2, dz2_g[0], 0, D)
+        def stage2b(c, i):
+            if i == 0:
+                wb[c] = bank([P, D], f"acc{c}")
+            mm(wb[c][:], dv_q[i], E5M2, P * c, h_q[i], E4M3, i == 0, i == 1)
+
+        def evac2b(copy, c):
+            copy(out=o1[:, c, :], in_=wb[c][:])
+
+        def store_out1(c):
+            nc.sync.dma_start(out=out_1[P * c : P * (c + 1), :], in_=o1[:, c, :])
+
+        relu_grad(0, y_raw[0][:, :, 0:256], 0, 256)
+        interleave(scopy, dz2_g[0], dz2[0], 0, 256)
+        relu_grad(0, y_raw[0][:, :, 256:512], 256, 512)
+        interleave(scopy, dz2_g[0], dz2[0], 256, 512)
+        quantize(dz2_q[0], E5M2, dz2_g[0], 0, 256)
+        quantize(dz2_q[0], E5M2, dz2_g[0], 256, 512)
         add_att(0, 0, 0, P)
         quantize(att_q[0, 0], E4M3, att_g[0, 0], 0, G)
-        stage1(0, 0, range(4))
-        relu_grad(1, y_raw[1][:], 0, D)
-        quantize(dz2_q[1], E5M2, dz2_g[1], 0, D)
+        stage1(0, 0, [0])
+        stage1(0, 0, [1])
+        stage1(0, 0, [2])
+        stage1(0, 0, [3])
+        relu_grad(1, y_raw[1][:, :, 0:256], 0, 256)
+        interleave(scopy, dz2_g[1], dz2[1], 0, 256)
+        relu_grad(1, y_raw[1][:, :, 256:512], 256, 512)
+        interleave(scopy, dz2_g[1], dz2[1], 256, 512)
+        quantize(dz2_q[1], E5M2, dz2_g[1], 0, 256)
         add_att(1, 0, 0, P)
-        quantize(att_q[1, 0], E4M3, att_g[1, 0], 0, G)
-        stage1(0, 1, range(4))
         interleave(scopy, wv_g, wv_raw, 0, D)
-        for t in range(4):
-            evac1(scopy, 0, t)
+        quantize(dz2_q[1], E5M2, dz2_g[1], 256, 512)
+        quantize(att_q[1, 0], E4M3, att_g[1, 0], 0, G)
+        stage1(0, 1, [0])
+        stage1(0, 1, [1])
+        stage1(0, 1, [2])
+        stage1(0, 1, [3])
         quantize(wv_q, E4M3, wv_g, 0, D)
-        add_att(0, 1, 0, P)
+        evac1(scopy, 0, 0)
+        evac1(scopy, 0, 1)
         turn(0, 0)
+        evac1(scopy, 0, 2)
+        evac1(scopy, 0, 3)
         turn(0, 1)
         turn_out(0, 0)
         turn_out(0, 1)
-        interleave(scopy, dv_g[0], dz1[0], 0, D)
+        add_att(0, 1, 0, P)
         quantize(dk_q[0], E5M2, dk_g[0], 0, 256)
-        quantize(att_q[0, 1], E4M3, att_g[0, 1], 0, G)
         stage2a(0, 0)
         stage2a(0, 1)
-        stage1(1, 0, range(4))
-        quantize(dk_q[0], E5M2, dk_g[0], 256, 512)
+        quantize(att_q[0, 1], E4M3, att_g[0, 1], 0, G)
+        stage1(1, 0, [0])
+        stage1(1, 0, [1])
+        stage1(1, 0, [2])
+        stage1(1, 0, [3])
         evac2a(0, 0)
+        quantize(dk_q[0], E5M2, dk_g[0], 256, 512)
         evac2a(0, 1)
+        store_out0(0, 0, 2)
         stage2a(0, 2)
         stage2a(0, 3)
-        add_att(1, 1, 0, 64)
-        quantize(dv_q[0], E5M2, dv_g[0], 0, D)
-        add_att(1, 1, 64, P)
-        evac2a(0, 2)
-        quantize(att_q[1, 1], E4M3, att_g[1, 1], 0, 256)
-        quantize(att_q[1, 1], E4M3, att_g[1, 1], 256, 512)
-        stage1(1, 1, range(4))
-        evac2a(0, 3)
-        store_out0(0, 0, 4)
         interleave(scopy, h_g[0], h_raw[0], 0, D)
+        interleave(scopy, dv_g[0], dz1[0], 0, D)
+        interleave(scopy, h_g[1], h_raw[1], 0, D)
+        add_att(1, 1, 0, P)
+        quantize(att_q[1, 1], E4M3, att_g[1, 1], 0, 256)
+        stage1(1, 1, [0])
+        stage1(1, 1, [1])
+        evac2a(0, 2)
+        quantize(att_q[1, 1], E4M3, att_g[1, 1], 256, 512)
+        stage1(1, 1, [2])
+        stage1(1, 1, [3])
         evac1(scopy, 1, 0)
-        evac1(vcopy, 1, 1)
-        evac1(scopy, 1, 2)
-        evac1(vcopy, 1, 3)
-        turn(1, 0)
-        turn(1, 1)
         quantize(h_q[0], E4M3, h_g[0], 0, D)
+        evac1(scopy, 1, 1)
+        turn(1, 0)
+        evac1(scopy, 1, 2)
         turn_out(1, 0)
-        turn_out(1, 1)
-        interleave(vcopy, dv_g[1], dz1[1], 0, 256)
+        evac2a(0, 3)
+        store_out0(0, 2, 4)
+        quantize(dv_q[0], E5M2, dv_g[0], 0, D)
+        evac1(vcopy, 1, 3)
+        turn(1, 1)
+        quantize(h_q[1], E4M3, h_g[1], 0, D)
         quantize(dk_q[1], E5M2, dk_g[1], 0, 256)
+        turn_out(1, 1)
+        stage2b(0, 0)
+        stage2b(1, 0)
         stage2a(1, 0)
         stage2a(1, 1)
-        interleave(scopy, h_g[1], h_raw[1], 0, D)
-        interleave(vcopy, dv_g[1], dz1[1], 256, 512)
-        quantize(dk_q[1], E5M2, dk_g[1], 256, 512)
-        quantize(dv_q[1], E5M2, dv_g[1], 0, D)
+        interleave(scopy, dv_g[1], dz1[1], 0, 256)
         evac2a(1, 0)
+        store_out0(1, 0, 1)
         evac2a(1, 1)
-        store_out0(1, 0, 2)
+        store_out0(1, 1, 2)
+        quantize(dk_q[1], E5M2, dk_g[1], 256, 512)
+        stage2b(2, 0)
+        stage2b(3, 0)
         stage2a(1, 2)
         stage2a(1, 3)
-        quantize(h_q[1], E4M3, h_g[1], 0, D)
+        interleave(scopy, dv_g[1], dz1[1], 256, 512)
+        quantize(dv_q[1], E5M2, dv_g[1], 0, 256)
+        stage2b(0, 1)
+        stage2b(1, 1)
         evac2a(1, 2)
+        store_out0(1, 2, 3)
+        evac2b(scopy, 0)
+        store_out1(0)
+        quantize(dv_q[1], E5M2, dv_g[1], 256, 512)
+        evac2b(scopy, 1)
+        store_out1(1)
+        stage2b(2, 1)
+        stage2b(3, 1)
         evac2a(1, 3)
-        store_out0(1, 2, 4)
-        for c in range(4):
-            wb = bank([P, D], f"acc{c}")
-            for i in range(2):
-                mm(wb[:], dv_q[i], E5M2, P * c, h_q[i], E4M3, i == 0, i == 1)
-            (scopy if c % 2 == 0 else vcopy)(out=o1[:, c, :], in_=wb[:])
-            if c % 2 == 1:
-                nc.sync.dma_start(
-                    out=out_1[P * (c - 1) : P * (c + 1), :].rearrange("(c p) w -> p c w", p=P), in_=o1[:, c - 1 : c + 1, :]
-                )
+        store_out0(1, 3, 4)
+        evac2b(scopy, 2)
+        store_out1(2)
+        evac2b(scopy, 3)
+        store_out1(3)

@@ -189,8 +189,8 @@ def tile_semanticgraph_pb_v_kernel(tc, q, k, h, cooccur, wv, bv, p, y, grad_out,
         relu_grad(0, y_raw[0][:, :, 256:512], 256, 512)
         interleave(scopy, dz2_g[0], dz2[0], 256, 512)
         quantize(dz2_q[0], E5M2, dz2_g[0], 0, 256)
-        quantize(dz2_q[0], E5M2, dz2_g[0], 256, 512)
         add_att(0, 0, 0, P)
+        quantize(dz2_q[0], E5M2, dz2_g[0], 256, 512)
         quantize(att_q[0, 0], E4M3, att_g[0, 0], 0, G)
         stage1(0, 0, [0])
         stage1(0, 0, [1])
@@ -202,92 +202,92 @@ def tile_semanticgraph_pb_v_kernel(tc, q, k, h, cooccur, wv, bv, p, y, grad_out,
         interleave(scopy, dz2_g[1], dz2[1], 256, 512)
         quantize(dz2_q[1], E5M2, dz2_g[1], 0, 256)
         add_att(1, 0, 0, P)
-        interleave(scopy, wv_g, wv_raw, 0, D)
         quantize(dz2_q[1], E5M2, dz2_g[1], 256, 512)
         quantize(att_q[1, 0], E4M3, att_g[1, 0], 0, G)
         stage1(0, 1, [0])
         stage1(0, 1, [1])
         stage1(0, 1, [2])
         stage1(0, 1, [3])
+        interleave(scopy, wv_g, wv_raw, 0, D)
         quantize(wv_q, E4M3, wv_g, 0, D)
+        add_att(0, 1, 0, P)
+        quantize(att_q[0, 1], E4M3, att_g[0, 1], 0, G)
         evac1(scopy, 0, 0)
         evac1(scopy, 0, 1)
         turn(0, 0)
         evac1(scopy, 0, 2)
-        evac1(scopy, 0, 3)
-        turn(0, 1)
+        interleave(scopy, h_g[0], h_raw[0], 0, D)
         turn_out(0, 0)
-        turn_out(0, 1)
-        add_att(0, 1, 0, P)
-        quantize(dk_q[0], E5M2, dk_g[0], 0, 256)
-        stage2a(0, 0)
-        stage2a(0, 1)
-        quantize(att_q[0, 1], E4M3, att_g[0, 1], 0, G)
+        evac1(scopy, 0, 3)
         stage1(1, 0, [0])
         stage1(1, 0, [1])
         stage1(1, 0, [2])
+        quantize(h_q[0], E4M3, h_g[0], 0, D)
+        quantize(dk_q[0], E5M2, dk_g[0], 0, 256)
+        stage2a(0, 0)
+        turn(0, 1)
+        stage2a(0, 1)
         stage1(1, 0, [3])
-        evac2a(0, 0)
-        quantize(dk_q[0], E5M2, dk_g[0], 256, 512)
-        evac2a(0, 1)
-        store_out0(0, 0, 2)
-        stage2a(0, 2)
-        stage2a(0, 3)
-        interleave(scopy, h_g[0], h_raw[0], 0, D)
         interleave(scopy, dv_g[0], dz1[0], 0, D)
+        turn_out(0, 1)
         interleave(scopy, h_g[1], h_raw[1], 0, D)
         add_att(1, 1, 0, P)
         quantize(att_q[1, 1], E4M3, att_g[1, 1], 0, 256)
         stage1(1, 1, [0])
         stage1(1, 1, [1])
-        evac2a(0, 2)
+        evac2a(0, 0)
         quantize(att_q[1, 1], E4M3, att_g[1, 1], 256, 512)
         stage1(1, 1, [2])
         stage1(1, 1, [3])
+        evac2a(0, 1)
+        store_out0(0, 0, 2)
+        quantize(dk_q[0], E5M2, dk_g[0], 256, 512)
         evac1(scopy, 1, 0)
-        quantize(h_q[0], E4M3, h_g[0], 0, D)
         evac1(scopy, 1, 1)
+        stage2a(0, 2)
+        stage2a(0, 3)
+        evac1(vcopy, 1, 2)
         turn(1, 0)
-        evac1(scopy, 1, 2)
-        turn_out(1, 0)
-        evac2a(0, 3)
-        store_out0(0, 2, 4)
-        quantize(dv_q[0], E5M2, dv_g[0], 0, D)
-        evac1(vcopy, 1, 3)
-        turn(1, 1)
+        evac1(scopy, 1, 3)
         quantize(h_q[1], E4M3, h_g[1], 0, D)
-        quantize(dk_q[1], E5M2, dk_g[1], 0, 256)
-        turn_out(1, 1)
+        quantize(dv_q[0], E5M2, dv_g[0], 0, D)
+        turn_out(1, 0)
+        turn(1, 1)
         stage2b(0, 0)
         stage2b(1, 0)
+        evac2a(0, 2)
+        quantize(dk_q[1], E5M2, dk_g[1], 0, 256)
+        evac2a(0, 3)
+        store_out0(0, 2, 4)
+        interleave(scopy, dv_g[1], dz1[1], 0, 256)
         stage2a(1, 0)
         stage2a(1, 1)
-        interleave(scopy, dv_g[1], dz1[1], 0, 256)
-        evac2a(1, 0)
-        store_out0(1, 0, 1)
-        evac2a(1, 1)
-        store_out0(1, 1, 2)
-        quantize(dk_q[1], E5M2, dk_g[1], 256, 512)
-        stage2b(2, 0)
-        stage2b(3, 0)
-        stage2a(1, 2)
-        stage2a(1, 3)
+        turn_out(1, 1)
         interleave(scopy, dv_g[1], dz1[1], 256, 512)
         quantize(dv_q[1], E5M2, dv_g[1], 0, 256)
+        evac2a(1, 0)
+        store_out0(1, 0, 1)
         stage2b(0, 1)
         stage2b(1, 1)
-        evac2a(1, 2)
-        store_out0(1, 2, 3)
+        stage2b(2, 0)
+        stage2b(3, 0)
+        evac2a(1, 1)
+        store_out0(1, 1, 2)
         evac2b(scopy, 0)
         store_out1(0)
+        quantize(dk_q[1], E5M2, dk_g[1], 256, 512)
+        stage2a(1, 2)
+        stage2a(1, 3)
         quantize(dv_q[1], E5M2, dv_g[1], 256, 512)
         evac2b(scopy, 1)
         store_out1(1)
         stage2b(2, 1)
         stage2b(3, 1)
-        evac2a(1, 3)
-        store_out0(1, 3, 4)
+        evac2a(1, 2)
+        store_out0(1, 2, 3)
         evac2b(scopy, 2)
         store_out1(2)
+        evac2a(1, 3)
+        store_out0(1, 3, 4)
         evac2b(scopy, 3)
         store_out1(3)

@@ -62,9 +62,9 @@ def tile_semanticgraph_pb_v_kernel(tc, q, k, h, cooccur, wv, bv, p, y, grad_out,
         wv_raw = load(rows(wv, 0, 0, D), [P, J, D], BF16, "wv_raw")
         c_raw[0, 1] = load_c(0, 1)
         p_raw[0, 1] = load_p(0, 1)
-        h_raw[0] = load(rows(h, 0, 0, D), [P, J, D], BF16, "h_raw0")
         c_raw[1, 1] = load_c(1, 1)
         p_raw[1, 1] = load_p(1, 1)
+        h_raw[0] = load(rows(h, 0, 0, D), [P, J, D], BF16, "h_raw0")
         h_raw[1] = load(rows(h, 1, 0, D), [P, J, D], BF16, "h_raw1")
 
         ident = sb([P, P], F32, "ident")
@@ -188,9 +188,8 @@ def tile_semanticgraph_pb_v_kernel(tc, q, k, h, cooccur, wv, bv, p, y, grad_out,
         interleave(scopy, dz2_g[0], dz2[0], 0, 256)
         relu_grad(0, y_raw[0][:, :, 256:512], 256, 512)
         interleave(scopy, dz2_g[0], dz2[0], 256, 512)
-        quantize(dz2_q[0], E5M2, dz2_g[0], 0, 256)
         add_att(0, 0, 0, P)
-        quantize(dz2_q[0], E5M2, dz2_g[0], 256, 512)
+        quantize(dz2_q[0], E5M2, dz2_g[0], 0, D)
         quantize(att_q[0, 0], E4M3, att_g[0, 0], 0, G)
         stage1(0, 0, [0])
         stage1(0, 0, [1])
@@ -200,9 +199,8 @@ def tile_semanticgraph_pb_v_kernel(tc, q, k, h, cooccur, wv, bv, p, y, grad_out,
         interleave(scopy, dz2_g[1], dz2[1], 0, 256)
         relu_grad(1, y_raw[1][:, :, 256:512], 256, 512)
         interleave(scopy, dz2_g[1], dz2[1], 256, 512)
-        quantize(dz2_q[1], E5M2, dz2_g[1], 0, 256)
         add_att(1, 0, 0, P)
-        quantize(dz2_q[1], E5M2, dz2_g[1], 256, 512)
+        quantize(dz2_q[1], E5M2, dz2_g[1], 0, D)
         quantize(att_q[1, 0], E4M3, att_g[1, 0], 0, G)
         stage1(0, 1, [0])
         stage1(0, 1, [1])
@@ -210,60 +208,60 @@ def tile_semanticgraph_pb_v_kernel(tc, q, k, h, cooccur, wv, bv, p, y, grad_out,
         stage1(0, 1, [3])
         interleave(scopy, wv_g, wv_raw, 0, D)
         quantize(wv_q, E4M3, wv_g, 0, D)
-        add_att(0, 1, 0, P)
-        quantize(att_q[0, 1], E4M3, att_g[0, 1], 0, G)
         evac1(scopy, 0, 0)
         evac1(scopy, 0, 1)
         turn(0, 0)
         evac1(scopy, 0, 2)
-        interleave(scopy, h_g[0], h_raw[0], 0, D)
-        turn_out(0, 0)
         evac1(scopy, 0, 3)
+        turn(0, 1)
+        turn_out(0, 0)
+        add_att(0, 1, 0, P)
+        interleave(scopy, dv_g[0], dz1[0], 0, D)
+        turn_out(0, 1)
+        quantize(att_q[0, 1], E4M3, att_g[0, 1], 0, G)
         stage1(1, 0, [0])
         stage1(1, 0, [1])
         stage1(1, 0, [2])
-        quantize(h_q[0], E4M3, h_g[0], 0, D)
+        stage1(1, 0, [3])
         quantize(dk_q[0], E5M2, dk_g[0], 0, 256)
         stage2a(0, 0)
-        turn(0, 1)
         stage2a(0, 1)
-        stage1(1, 0, [3])
-        interleave(scopy, dv_g[0], dz1[0], 0, D)
-        turn_out(0, 1)
         interleave(scopy, h_g[1], h_raw[1], 0, D)
         add_att(1, 1, 0, P)
+        quantize(dk_q[0], E5M2, dk_g[0], 256, 512)
         quantize(att_q[1, 1], E4M3, att_g[1, 1], 0, 256)
         stage1(1, 1, [0])
         stage1(1, 1, [1])
-        evac2a(0, 0)
         quantize(att_q[1, 1], E4M3, att_g[1, 1], 256, 512)
         stage1(1, 1, [2])
         stage1(1, 1, [3])
-        evac2a(0, 1)
-        store_out0(0, 0, 2)
-        quantize(dk_q[0], E5M2, dk_g[0], 256, 512)
         evac1(scopy, 1, 0)
         evac1(scopy, 1, 1)
+        evac1(scopy, 1, 2)
+        evac1(scopy, 1, 3)
+        interleave(vcopy, h_g[0], h_raw[0], 0, D)
+        quantize(dv_q[0], E5M2, dv_g[0], 0, D)
+        quantize(h_q[0], E4M3, h_g[0], 0, D)
+        turn(1, 0)
+        evac2a(0, 0)
+        evac2a(0, 1)
+        store_out0(0, 0, 2)
         stage2a(0, 2)
         stage2a(0, 3)
-        evac1(vcopy, 1, 2)
-        turn(1, 0)
-        evac1(scopy, 1, 3)
-        quantize(h_q[1], E4M3, h_g[1], 0, D)
-        quantize(dv_q[0], E5M2, dv_g[0], 0, D)
         turn_out(1, 0)
         turn(1, 1)
         stage2b(0, 0)
         stage2b(1, 0)
+        quantize(h_q[1], E4M3, h_g[1], 0, D)
         evac2a(0, 2)
+        store_out0(0, 2, 3)
         quantize(dk_q[1], E5M2, dk_g[1], 0, 256)
-        evac2a(0, 3)
-        store_out0(0, 2, 4)
         interleave(scopy, dv_g[1], dz1[1], 0, 256)
         stage2a(1, 0)
+        evac2a(0, 3)
+        store_out0(0, 3, 4)
         stage2a(1, 1)
         turn_out(1, 1)
-        interleave(scopy, dv_g[1], dz1[1], 256, 512)
         quantize(dv_q[1], E5M2, dv_g[1], 0, 256)
         evac2a(1, 0)
         store_out0(1, 0, 1)
@@ -271,22 +269,23 @@ def tile_semanticgraph_pb_v_kernel(tc, q, k, h, cooccur, wv, bv, p, y, grad_out,
         stage2b(1, 1)
         stage2b(2, 0)
         stage2b(3, 0)
+        interleave(scopy, dv_g[1], dz1[1], 256, 512)
         evac2a(1, 1)
         store_out0(1, 1, 2)
+        quantize(dv_q[1], E5M2, dv_g[1], 256, 512)
         evac2b(scopy, 0)
         store_out1(0)
         quantize(dk_q[1], E5M2, dk_g[1], 256, 512)
-        stage2a(1, 2)
-        stage2a(1, 3)
-        quantize(dv_q[1], E5M2, dv_g[1], 256, 512)
         evac2b(scopy, 1)
         store_out1(1)
         stage2b(2, 1)
+        stage2a(1, 2)
         stage2b(3, 1)
-        evac2a(1, 2)
-        store_out0(1, 2, 3)
         evac2b(scopy, 2)
         store_out1(2)
+        evac2a(1, 2)
+        store_out0(1, 2, 3)
+        stage2a(1, 3)
         evac2a(1, 3)
         store_out0(1, 3, 4)
         evac2b(scopy, 3)

from contextlib import ExitStack

import concourse.mybir as mybir
from concourse.masks import make_identity

N = 1024
D = 512
P = 128
J = 4
G = 512

F32 = mybir.dt.float32
BF16 = mybir.dt.bfloat16
U32 = mybir.dt.uint32
U8 = mybir.dt.uint8
E4M3 = mybir.dt.float8_e4m3fn_x4
E5M2 = mybir.dt.float8_e5m2_x4
ALU = mybir.AluOpType

FLOPS = 2 * N * N * D + 2 * 2 * N * D * D
BYTES = N * D * 2 * 2 + N * N * 2 + D * D * 2 + N * N * 4 + N * D * 4 + N * D * 4 + D * D * 4


def tile_semanticgraph_pb_v_kernel(tc, q, k, h, cooccur, wv, bv, p, y, grad_out, out_0, out_1):
    nc = tc.nc
    with ExitStack() as ctx:
        keep = ctx.enter_context(tc.tile_pool(name="keep", bufs=1))
        psum = ctx.enter_context(tc.psum_pool(name="psum", bufs=1))

        def sb(shape, dtype, name):
            return keep.tile(shape, dtype, name=name, align_bytes=64)

        def bank(shape, name):
            return psum.tile(shape, F32, name=name)

        ctx.enter_context(tc.manual_schedule())

        def load(ap, shape, dtype, name):
            t = sb(shape, dtype, name)
            nc.sync.dma_start(out=t[:], in_=ap)
            return t

        def rows(ap, i, c0, c1):
            return ap[G * i : G * (i + 1), c0:c1].rearrange("(p j) w -> p j w", j=J)

        def load_p(i, hf):
            return load(rows(p, i, G * hf, G * (hf + 1)), [P, J, G], F32, f"p_{i}{hf}")

        def load_c(i, hf):
            return load(rows(cooccur, i, G * hf, G * (hf + 1)), [P, J, G], BF16, f"c_{i}{hf}")[:]

        g_raw, y_raw, p_raw, c_raw = {}, {}, {}, {}
        h_raw = {}
        y_raw[0] = load(rows(y, 0, 0, D), [P, J, D], F32, "y_0")
        g_raw[0] = load(rows(grad_out, 0, 0, D), [P, J, D], BF16, "g_0")
        c_raw[0, 0] = load_c(0, 0)
        p_raw[0, 0] = load_p(0, 0)
        y_raw[1] = load(rows(y, 1, 0, D), [P, J, D], F32, "y_1")
        g_raw[1] = load(rows(grad_out, 1, 0, D), [P, J, D], BF16, "g_1")
        c_raw[1, 0] = load_c(1, 0)
        p_raw[1, 0] = load_p(1, 0)
        wv_raw = load(rows(wv, 0, 0, D), [P, J, D], BF16, "wv_raw")
        c_raw[0, 1] = load_c(0, 1)
        p_raw[0, 1] = load_p(0, 1)
        c_raw[1, 1] = load_c(1, 1)
        p_raw[1, 1] = load_p(1, 1)
        h_raw[0] = load(rows(h, 0, 0, D), [P, J, D], BF16, "h_raw0")
        h_raw[1] = load(rows(h, 1, 0, D), [P, J, D], BF16, "h_raw1")

        ident = sb([P, P], F32, "ident")
        make_identity(nc, ident[:])

        def operand(width, name):
            return (sb([P, width], U32, name + "_codes"), sb([P, width], U8, name + "_scales"))

        def quantize(op, fmt, grouped, c0, c1):
            codes, scales = op
            nc.vector.quantize_mx(
                out=codes[:, c0:c1].bitcast(fmt), scales=scales[:, c0:c1], in_=grouped[:, J * c0 : J * c1]
            )

        dz2 = [sb([P, J, D], BF16, f"dz2_{i}") for i in range(2)]
        dz2_g = [sb([P, D * J], BF16, f"dz2_g{i}") for i in range(2)]
        dz2_q = [operand(D, f"dz2_q{i}") for i in range(2)]
        att_g = {(i, hf): sb([P, G * J], BF16, f"att_g{i}{hf}") for i in range(2) for hf in range(2)}
        att_q = {(i, hf): operand(G, f"att_q{i}{hf}") for i in range(2) for hf in range(2)}
        wv_g = sb([P, D * J], BF16, "wv_g")
        wv_q = operand(D, "wv_q")
        h_g = [sb([P, D * J], BF16, f"h_g{i}") for i in range(2)]
        h_q = [operand(D, f"h_q{i}") for i in range(2)]
        dz1 = [sb([P, J, D], BF16, f"dz1_{hf}") for hf in range(2)]
        dk_g = [sb([P, G * J], BF16, f"dk_g{hf}") for hf in range(2)]
        dk_q = [operand(G, f"dk_q{hf}") for hf in range(2)]
        dv_g = [sb([P, D * J], BF16, f"dv_g{hf}") for hf in range(2)]
        dv_q = [operand(D, f"dv_q{hf}") for hf in range(2)]
        o0 = [sb([P, J, D], F32, f"o0_{hf}") for hf in range(2)]
        o1 = sb([P, J, D], F32, "o1")

        def relu_grad(i, yt, c0, c1):
            nc.vector.scalar_tensor_tensor(
                out=dz2[i][:, :, c0:c1],
                in0=yt,
                scalar=0.0,
                in1=g_raw[i][:, :, c0:c1],
                op0=ALU.is_gt,
                op1=ALU.mult,
            )


        def add_att(i, hf, m0, m1):
            nc.vector.tensor_tensor(
                out=att_g[i, hf][:].rearrange("p (t m j) -> p m j t", t=4, j=J)[:, m0:m1],
                in0=p_raw[i, hf][:].rearrange("p j (m t) -> p m j t", t=4)[:, m0:m1],
                in1=c_raw[i, hf].rearrange("p j (m t) -> p m j t", t=4)[:, m0:m1],
                op=ALU.add,
            )

        def interleave(engine_copy, dst, src, c0, c1):
            engine_copy(
                out=dst[:, J * c0 : J * c1].rearrange("p (c i j) -> p c j i", i=4, j=J),
                in_=src[:, :, c0:c1].rearrange("p j (c i) -> p c j i", i=4),
            )

        def mm(out, a, a_fmt, a0, b, b_fmt, start, stop):
            nc.tensor.matmul_mx(
                out=out,
                lhsT=a[0][:, a0 : a0 + P].bitcast(a_fmt),
                lhsT_scale=a[1][:, a0 : a0 + P],
                rhs=b[0][:].bitcast(b_fmt),
                rhs_scale=b[1][:],
                start=start,
                stop=stop,
            )

        acc = {}

        def stage1(hf, i, ts):
            for t in ts:
                if i == 0:
                    acc[hf, t] = bank([P, D], f"acc{t}")
                mm(acc[hf, t][:], att_q[i, hf], E4M3, P * t, dz2_q[i], E5M2, i == 0, i == 1)

        def evac1(copy, hf, t):
            copy(out=dz1[hf][:, t, :], in_=acc[hf, t][:])

        tb = {}

        def turn(hf, b):
            tb[hf, b] = bank([P, 2, 2, P], f"turn{b}")
            for a in range(2):
                words = dz1[hf][:, 2 * b + a, :].bitcast(F32)
                for u in range(2):
                    nc.tensor.transpose(tb[hf, b][:, a, u, :], words[:, u::2], ident[:])

        def turn_out(hf, b):
            nc.scalar.copy(
                out=dk_g[hf][:, 2 * P * J * b : 2 * P * J * (b + 1)].bitcast(F32).rearrange("p (a r u) -> p a r u", a=2, u=2),
                in_=tb[hf, b][:].rearrange("p a u r -> p a r u"),
            )

        ob = {}

        def stage2a(hf, t):
            ob[hf, t] = bank([P, D], f"turn{t - 2}" if (hf, t // 2) == (1, 1) else f"ob{t % 2}")
            mm(ob[hf, t][:], dk_q[hf], E5M2, P * t, wv_q, E4M3, True, True)

        def evac2a(hf, t):
            nc.vector.tensor_tensor(out=o0[hf][:, t, :], in0=ob[hf, t][:], in1=g_raw[hf][:, t, :], op=ALU.add)

        def store_out0(hf, t0, t1):
            nc.sync.dma_start(out=rows(out_0, hf, 0, D)[:, t0:t1, :], in_=o0[hf][:, t0:t1, :])

        vcopy, scopy = nc.vector.tensor_copy, nc.scalar.copy
        wb = {}

        def stage2b(c, i):
            if i == 0:
                wb[c] = bank([P, D], f"acc{c}")
            mm(wb[c][:], dv_q[i], E5M2, P * c, h_q[i], E4M3, i == 0, i == 1)

        def evac2b(copy, c):
            copy(out=o1[:, c, :], in_=wb[c][:])

        def store_out1(c):
            nc.sync.dma_start(out=out_1[P * c : P * (c + 1), :], in_=o1[:, c, :])

        relu_grad(0, y_raw[0][:, :, 0:256], 0, 256)
        interleave(scopy, dz2_g[0], dz2[0], 0, 256)
        relu_grad(0, y_raw[0][:, :, 256:512], 256, 512)
        interleave(scopy, dz2_g[0], dz2[0], 256, 512)
        add_att(0, 0, 0, P)
        quantize(dz2_q[0], E5M2, dz2_g[0], 0, D)
        quantize(att_q[0, 0], E4M3, att_g[0, 0], 0, G)
        stage1(0, 0, [0])
        stage1(0, 0, [1])
        stage1(0, 0, [2])
        stage1(0, 0, [3])
        relu_grad(1, y_raw[1][:, :, 0:256], 0, 256)
        interleave(scopy, dz2_g[1], dz2[1], 0, 256)
        relu_grad(1, y_raw[1][:, :, 256:512], 256, 512)
        interleave(scopy, dz2_g[1], dz2[1], 256, 512)
        add_att(1, 0, 0, P)
        quantize(dz2_q[1], E5M2, dz2_g[1], 0, D)
        quantize(att_q[1, 0], E4M3, att_g[1, 0], 0, G)
        stage1(0, 1, [0])
        stage1(0, 1, [1])
        stage1(0, 1, [2])
        stage1(0, 1, [3])
        interleave(scopy, wv_g, wv_raw, 0, D)
        quantize(wv_q, E4M3, wv_g, 0, D)
        evac1(scopy, 0, 0)
        evac1(scopy, 0, 1)
        turn(0, 0)
        evac1(scopy, 0, 2)
        evac1(scopy, 0, 3)
        turn(0, 1)
        turn_out(0, 0)
        add_att(0, 1, 0, P)
        interleave(scopy, dv_g[0], dz1[0], 0, D)
        turn_out(0, 1)
        quantize(att_q[0, 1], E4M3, att_g[0, 1], 0, G)
        stage1(1, 0, [0])
        stage1(1, 0, [1])
        stage1(1, 0, [2])
        stage1(1, 0, [3])
        quantize(dk_q[0], E5M2, dk_g[0], 0, 256)
        stage2a(0, 0)
        stage2a(0, 1)
        interleave(scopy, h_g[1], h_raw[1], 0, D)
        add_att(1, 1, 0, P)
        quantize(dk_q[0], E5M2, dk_g[0], 256, 512)
        quantize(att_q[1, 1], E4M3, att_g[1, 1], 0, 256)
        stage1(1, 1, [0])
        stage1(1, 1, [1])
        quantize(att_q[1, 1], E4M3, att_g[1, 1], 256, 512)
        stage1(1, 1, [2])
        stage1(1, 1, [3])
        evac1(scopy, 1, 0)
        evac1(scopy, 1, 1)
        evac1(scopy, 1, 2)
        evac1(scopy, 1, 3)
        interleave(vcopy, h_g[0], h_raw[0], 0, D)
        quantize(dv_q[0], E5M2, dv_g[0], 0, D)
        quantize(h_q[0], E4M3, h_g[0], 0, D)
        turn(1, 0)
        evac2a(0, 0)
        evac2a(0, 1)
        store_out0(0, 0, 2)
        stage2a(0, 2)
        stage2a(0, 3)
        turn_out(1, 0)
        turn(1, 1)
        stage2b(0, 0)
        stage2b(1, 0)
        quantize(h_q[1], E4M3, h_g[1], 0, D)
        evac2a(0, 2)
        store_out0(0, 2, 3)
        quantize(dk_q[1], E5M2, dk_g[1], 0, 256)
        interleave(scopy, dv_g[1], dz1[1], 0, 256)
        stage2a(1, 0)
        evac2a(0, 3)
        store_out0(0, 3, 4)
        stage2a(1, 1)
        turn_out(1, 1)
        quantize(dv_q[1], E5M2, dv_g[1], 0, 256)
        evac2a(1, 0)
        store_out0(1, 0, 1)
        stage2b(0, 1)
        stage2b(1, 1)
        stage2b(2, 0)
        stage2b(3, 0)
        interleave(scopy, dv_g[1], dz1[1], 256, 512)
        evac2a(1, 1)
        store_out0(1, 1, 2)
        quantize(dv_q[1], E5M2, dv_g[1], 256, 512)
        evac2b(scopy, 0)
        store_out1(0)
        quantize(dk_q[1], E5M2, dk_g[1], 256, 512)
        evac2b(scopy, 1)
        store_out1(1)
        stage2b(2, 1)
        stage2a(1, 2)
        stage2b(3, 1)
        evac2b(scopy, 2)
        store_out1(2)
        evac2a(1, 2)
        store_out0(1, 2, 3)
        stage2a(1, 3)
        evac2a(1, 3)
        store_out0(1, 3, 4)
        evac2b(scopy, 3)
        store_out1(3)
